import numpy as np
import ml_dtypes


def mxq(x, axis, fmt="e4m3"):
    dtype, down = {"e4m3": (ml_dtypes.float8_e4m3fn, 7), "e5m2": (ml_dtypes.float8_e5m2, 14)}[fmt]
    v = np.moveaxis(np.asarray(x, np.float32).astype(ml_dtypes.bfloat16).astype(np.float64), axis, -1)
    blocks = v.reshape(v.shape[:-1] + (-1, 32))
    amax = np.abs(blocks).max(-1, keepdims=True)
    byte = np.maximum(np.where(amax > 0, np.frexp(amax)[1] - 1 + 127, 0) - down, 1)
    scale = np.exp2(byte - 127.0)
    codes = (blocks / scale).astype(np.float32).astype(dtype).astype(np.float64)
    return np.moveaxis((codes * scale).reshape(v.shape), -1, axis)


WIDE = False


def mx_kscale(k):
    if not WIDE:
        return np.ones(k)
    levels = np.array([10, -10, 5, -5, 0])
    a = np.random.permutation(np.resize(levels, k // 512 * 4)).reshape(k // 512, 4)
    idx = np.arange(k)
    return np.exp2(a[idx // 512, idx % 128 // 32])


BF16 = ml_dtypes.bfloat16


def bf(x):
    return np.asarray(x, np.float32).astype(BF16)


def f64(x):
    return np.asarray(x).astype(np.float64)


B, S, D_IN, D_OUT, GROUP_SIZE = 4, 2048, 1024, 512, 128
EPS = 1e-8


def group_kscale(k, g):
    u = np.unique(mx_kscale(k))
    n = len(u)
    lv = u[[n - 1 - i // 2 if i % 2 == 0 else i // 2 for i in range(n)]]
    return np.repeat(lv[np.arange(k // g) % n], g)


def ternary_quantize_groupwise(w, group_size=GROUP_SIZE, eps=EPS):
    orig_shape = w.shape
    last = orig_shape[-1]
    pad = (-last) % group_size
    if pad > 0:
        w = np.pad(w, [(0, 0)] * (w.ndim - 1) + [(0, pad)])
    num_groups = w.shape[-1] // group_size
    wg = w.reshape(-1, num_groups, group_size)
    scale = np.maximum(np.mean(np.abs(wg), axis=-1, keepdims=True), eps)
    wn = wg / scale
    q = np.where(wn > 0.5, 1.0, np.where(wn < -0.5, -1.0, 0.0))
    wq = (q * scale).reshape(w.shape)
    if pad > 0:
        wq = wq[..., :last]
    return wq.reshape(orig_shape)


def quantize_with_ste(w_real, group_size=GROUP_SIZE):
    w_q = ternary_quantize_groupwise(w_real, group_size=group_size)
    return w_real + (w_q - w_real)


def setup_inputs():
    s = group_kscale(D_IN, GROUP_SIZE)
    bound_w = 2.0 / np.sqrt(D_IN)
    return {"x": bf(np.random.standard_normal((B, S, D_IN)) * s),
            "weight": bf(np.random.uniform(-bound_w, bound_w, (D_OUT, D_IN)) / s),
            "bias": bf(np.random.uniform(-0.5, 0.5, D_OUT))}


def reference(x, weight, bias):
    w_q = quantize_with_ste(f64(weight), group_size=GROUP_SIZE)
    return (mxq(f64(x), 2, "e4m3") @ mxq(w_q, 1, "e4m3").T) + f64(bias)

@@ -1,0 +1,274 @@
+from contextlib import ExitStack
+
+import concourse.mybir as mybir
+from concourse.masks import make_identity
+
+F32 = mybir.dt.float32
+BF16 = mybir.dt.bfloat16
+U32 = mybir.dt.uint32
+U8 = mybir.dt.uint8
+I32 = mybir.dt.int32
+FP8X4 = mybir.dt.float8_e4m3fn_x4
+ALU = mybir.AluOpType
+AX = mybir.AxisListType
+
+P = 128
+TOKENS = 4 * 2048
+D_IN = 1024
+D_OUT = 512
+GROUP = 128
+GROUPS = D_IN // GROUP
+EPS = 1e-8
+K_PASS = 4 * P
+PASSES = D_IN // K_PASS
+WORDS = D_IN // 2
+TILES = 4
+BUNCH = P * TILES
+BUNCHES = TOKENS // BUNCH
+OUT_TILES = D_OUT // P
+
+LAG = 7
+SORTED = 2
+POOL_TILES = 1
+X_BUFS = 4
+G_BUFS = LAG + 1
+C_BUFS = LAG + 2
+R_BUFS = 3
+WT_AFTER = (0, 1, 2, 4)
+
+FLOPS = 2 * TOKENS * D_IN * D_OUT
+
+
+def tile_bitlinear_t_kernel(tc, x, weight, bias, out):
+    nc = tc.nc
+    x_rows = x.flatten_outer_dims()
+    out_rows = out.flatten_outer_dims()
+
+    with ExitStack() as ctx:
+        ctx.enter_context(tc.manual_schedule())
+        const = ctx.enter_context(tc.tile_pool(name="const", bufs=1))
+        wpool = ctx.enter_context(tc.tile_pool(name="wpool", bufs=1))
+        wtmp = ctx.enter_context(tc.tile_pool(name="wtmp", bufs=2))
+        xpool = ctx.enter_context(tc.tile_pool(name="xpool", bufs=X_BUFS))
+        spool = ctx.enter_context(tc.tile_pool(name="spool", bufs=2 * max(SORTED, 1)))
+        gpool = ctx.enter_context(tc.tile_pool(name="gpool", bufs=G_BUFS))
+        cpool = ctx.enter_context(tc.tile_pool(name="cpool", bufs=C_BUFS))
+        opool = ctx.enter_context(tc.tile_pool(name="opool", bufs=R_BUFS))
+        rpool = ctx.enter_context(tc.tile_pool(name="rpool", bufs=2))
+        psum = ctx.enter_context(tc.psum_pool(name="psum", bufs=8))
+
+        ident = const.tile([P, P], F32, name="ident")
+        make_identity(nc, ident[:])
+        ident_bf = const.tile([P, P], BF16, name="ident_bf")
+        make_identity(nc, ident_bf[:])
+        ones = const.tile([P, P], BF16, name="ones")
+        nc.vector.memset(ones[:], 1.0)
+        bias_pad = const.tile([P, D_OUT], BF16, name="bias_pad")
+        nc.vector.memset(bias_pad[:], 0.0)
+        nc.scalar.dma_start(out=bias_pad[0:1, :], in_=bias.rearrange("(o n) -> o n", o=1))
+        bias_all = const.tile([P, D_OUT], F32, name="bias_all")
+
+        x_tiles = {}
+        sorted_tiles = {}
+        grouped_tiles = {}
+        code_tiles = {}
+
+        def x_view(b):
+            return x_rows[b * BUNCH : (b + 1) * BUNCH, :].rearrange("(p t) k -> p t k", t=TILES)
+
+        def out_view(b):
+            return out_rows[b * BUNCH : (b + 1) * BUNCH, :].rearrange("(p t) n -> p t n", t=TILES)
+
+        def load(b, pieces):
+            xs = xpool.tile([P, TILES, D_IN], BF16, name="xs")
+            step = TILES // pieces
+            for t in range(0, TILES, step):
+                nc.sync.dma_start(out=xs[:, t : t + step, :], in_=x_view(b)[:, t : t + step, :])
+            x_tiles[b] = xs
+
+        def is_sorted(b, t):
+            return b > LAG and t >= TILES - SORTED
+
+        def sort_words(b):
+            for t in range(TILES):
+                if is_sorted(b, t):
+                    xsort = spool.tile([P, WORDS], F32, name="xsort")
+                    nc.scalar.copy(
+                        out=xsort[:].rearrange("p (g u i) -> p g u i", g=PASSES, u=2),
+                        in_=x_tiles[b][:, t, :].bitcast(F32).rearrange("p (g i u) -> p g u i", g=PASSES, u=2),
+                    )
+                    sorted_tiles[(b, t)] = xsort
+
+        def transposes(b):
+            banks = []
+            for t in range(TILES):
+                bank = psum.tile([P, WORDS], F32, name="bank")
+                if is_sorted(b, t):
+                    planes = sorted_tiles[(b, t)][:].rearrange("p (g u i) -> p g u i", g=PASSES, u=2)
+                else:
+                    planes = x_tiles[b][:, t, :].bitcast(F32).rearrange("p (g i u) -> p g u i", g=PASSES, u=2)
+                for g in range(PASSES):
+                    for u in range(2):
+                        plane = 2 * g + u
+                        nc.tensor.transpose(bank[:, plane * P : (plane + 1) * P], planes[:, g, u, :], ident[:])
+                banks.append(bank)
+            return banks
+
+        def evacuate(b, banks):
+            grouped = gpool.tile([P, TILES * D_IN], BF16, name="grouped", align_bytes=64)
+            for t in range(TILES):
+                dst = grouped[:, t * D_IN : (t + 1) * D_IN].bitcast(F32).rearrange("p (g r u) -> p g r u", g=PASSES, u=2)
+                src = banks[t][:].rearrange("p (g u r) -> p g r u", g=PASSES, u=2)
+                nc.scalar.copy(out=dst, in_=src)
+            grouped_tiles[b] = grouped
+
+        def quantise(b):
+            codes = cpool.tile([P, TILES * PASSES * P], U32, name="codes", align_bytes=64)
+            scales = cpool.tile([P, TILES * PASSES * P], U8, name="scales", align_bytes=64)
+            nc.vector.quantize_mx(out=codes[:].bitcast(FP8X4), scales=scales[:], in_=grouped_tiles[b][:])
+            code_tiles[b] = (codes, scales)
+
+        w_sb = wpool.tile([P, OUT_TILES, D_IN], BF16, name="w_sb")
+        w_view = weight.rearrange("(a p) k -> p a k", p=P)
+        sums = wpool.tile([P, OUT_TILES * GROUPS], F32, name="sums")
+        scl = wpool.tile([P, OUT_TILES * GROUPS], F32, name="scl")
+        thr = wpool.tile([P, OUT_TILES * GROUPS], F32, name="thr")
+        scl2 = wpool.tile([P, OUT_TILES * GROUPS], F32, name="scl2")
+        w_grouped = wpool.tile([P, PASSES * D_OUT * 4], BF16, name="w_grouped", align_bytes=64)
+        w_codes = wpool.tile([P, PASSES * D_OUT], U32, name="w_codes", align_bytes=64)
+        w_scales = wpool.tile([P, PASSES * D_OUT], U8, name="w_scales", align_bytes=64)
+        w_grouped_values = w_grouped[:].rearrange("p (g o t) -> p g o t", g=PASSES, t=4)
+        wq_tiles = {}
+        wt_banks = {}
+
+        def load_weights(a):
+            nc.sync.dma_start(out=w_sb[:, a, :], in_=w_view[:, a, :])
+
+        def ternary(a):
+            these = slice(a * GROUPS, (a + 1) * GROUPS)
+            mag = wtmp.tile([P, D_IN], BF16, name="mag")
+            nc.vector.tensor_scalar(
+                out=mag[:].bitcast(I32), in0=w_sb[:, a, :].bitcast(I32), scalar1=0x7FFF7FFF, scalar2=None, op0=ALU.bitwise_and
+            )
+            nc.vector.tensor_reduce(
+                out=sums[:, these], in_=mag[:].rearrange("p (j i) -> p j i", j=GROUPS), axis=AX.X, op=ALU.add
+            )
+            nc.vector.tensor_scalar(
+                out=scl[:, these], in0=sums[:, these], scalar1=1.0 / GROUP, scalar2=EPS, op0=ALU.mult, op1=ALU.max
+            )
+            nc.vector.tensor_scalar(out=thr[:, these], in0=scl[:, these], scalar1=0.5, scalar2=None, op0=ALU.mult)
+            nc.vector.tensor_scalar(out=scl2[:, these], in0=scl[:, these], scalar1=2.0, scalar2=None, op0=ALU.mult)
+            half_sign = wtmp.tile([P, D_IN], BF16, name="half_sign")
+            nc.vector.tensor_scalar(
+                out=half_sign[:], in0=w_sb[:, a, :], scalar1=0.0, scalar2=0.5, op0=ALU.is_ge, op1=ALU.subtract
+            )
+            kept = wtmp.tile([P, D_IN], BF16, name="kept")
+            for j in range(GROUPS):
+                c = a * GROUPS + j
+                cols = slice(j * GROUP, (j + 1) * GROUP)
+                nc.vector.tensor_scalar(
+                    out=kept[:, cols], in0=mag[:, cols], scalar1=thr[:, c : c + 1], scalar2=scl2[:, c : c + 1],
+                    op0=ALU.is_gt, op1=ALU.mult,
+                )
+            wq = wtmp.tile([P, D_IN], BF16, name="wq")
+            nc.vector.tensor_tensor(
+                out=wq[:].rearrange("p (g t i) -> p g t i", g=PASSES, t=4),
+                in0=kept[:].rearrange("p (g i t) -> p g t i", g=PASSES, t=4),
+                in1=half_sign[:].rearrange("p (g i t) -> p g t i", g=PASSES, t=4),
+                op=ALU.mult,
+            )
+            wq_tiles[a] = wq
+
+        def transpose_weights(a):
+            wt = psum.tile([P, D_IN], BF16, name="wt", tag="bank")
+            for plane in range(PASSES * 4):
+                cols = slice(plane * P, (plane + 1) * P)
+                nc.tensor.transpose(wt[:, cols], wq_tiles[a][:, cols], ident_bf[:])
+            nc.scalar.copy(
+                out=w_grouped_values[:, :, a * P : (a + 1) * P, :],
+                in_=wt[:].rearrange("p (g t r) -> p g r t", g=PASSES, t=4),
+            )
+
+        def quantise_weights(a):
+            for g in range(PASSES):
+                lo = g * D_OUT + a * P
+                nc.vector.quantize_mx(
+                    out=w_codes[:, lo : lo + P].bitcast(FP8X4),
+                    scales=w_scales[:, lo : lo + P],
+                    in_=w_grouped[:, 4 * lo : 4 * (lo + P)],
+                )
+
+        def multiply(i):
+            codes, scales = code_tiles[i]
+            banks = []
+            for t in range(TILES):
+                acc = psum.tile([P, D_OUT], F32, name="acc", tag="bank")
+                for g in range(PASSES):
+                    cols = slice((t * PASSES + g) * P, (t * PASSES + g + 1) * P)
+                    outs = slice(g * D_OUT, (g + 1) * D_OUT)
+                    nc.tensor.matmul_mx(
+                        out=acc[:],
+                        lhsT=codes[:, cols].bitcast(FP8X4),
+                        lhsT_scale=scales[:, cols],
+                        rhs=w_codes[:, outs].bitcast(FP8X4),
+                        rhs_scale=w_scales[:, outs],
+                        start=(g == 0),
+                        stop=(g == PASSES - 1),
+                    )
+                banks.append(acc)
+            return banks
+
+        load_weights(0)
+        load(0, TILES)
+        load_weights(1)
+        load(1, 1)
+        load_weights(2)
+        load(2, 1)
+        load_weights(3)
+        load(3, 1)
+
+        next_q = 0
+        for s in range(BUNCHES + LAG):
+            i = s - LAG
+            if s < BUNCHES:
+                banks = transposes(s)
+                if s + X_BUFS < BUNCHES:
+                    load(s + X_BUFS, 1)
+                evacuate(s, banks)
+            if s == 0:
+                bias_bank = psum.tile([P, D_OUT], F32, name="bias_bank", tag="bank")
+                nc.tensor.matmul(out=bias_bank[:], lhsT=ones[:], rhs=bias_pad[:], start=True, stop=True)
+                nc.scalar.copy(out=bias_all[:], in_=bias_bank[:])
+            if s == 0:
+                ternary(0)
+            for a in range(OUT_TILES):
+                if WT_AFTER[a] == s:
+                    transpose_weights(a)
+                    if a + 1 < OUT_TILES:
+                        ternary(a + 1)
+                    else:
+                        quantise(0)
+                        quantise(1)
+                        next_q = 2
+                    quantise_weights(a)
+            if i >= 0:
+                accs = multiply(i)
+                for n in range(2):
+                    if next_q < min(s, BUNCHES):
+                        quantise(next_q)
+                        next_q += 1
+                result = opool.tile([P, TILES, D_OUT], F32, name="result")
+                last = i == BUNCHES - 1
+                for t in range(TILES):
+                    if t < POOL_TILES:
+                        raw = rpool.tile([P, D_OUT], F32, name="raw")
+                        nc.scalar.copy(out=raw[:], in_=accs[t][:])
+                        nc.gpsimd.tensor_tensor(out=result[:, t, :], in0=raw[:], in1=bias_all[:], op=ALU.add)
+                    else:
+                        nc.vector.tensor_tensor(out=result[:, t, :], in0=accs[t][:], in1=bias_all[:], op=ALU.add)
+                    if last:
+                        nc.sync.dma_start(out=out_view(i)[:, t, :], in_=result[:, t, :])
+                if not last:
+                    nc.sync.dma_start(out=out_view(i), in_=result[:])
+            if s + 1 < BUNCHES:
+                sort_words(s + 1)

@@ -30,6 +30,7 @@ OUT_TILES = D_OUT // P
 LAG = 7
 SORTED = 2
 POOL_TILES = 1
+GRAN = 2
 X_BUFS = 4
 G_BUFS = LAG + 1
 C_BUFS = LAG + 2
@@ -99,9 +100,9 @@ def tile_bitlinear_t_kernel(tc, x, weight, bias, out):
                     )
                     sorted_tiles[(b, t)] = xsort
 
-        def transposes(b):
+        def transposes(b, tiles):
             banks = []
-            for t in range(TILES):
+            for t in tiles:
                 bank = psum.tile([P, WORDS], F32, name="bank")
                 if is_sorted(b, t):
                     planes = sorted_tiles[(b, t)][:].rearrange("p (g u i) -> p g u i", g=PASSES, u=2)
@@ -114,13 +115,15 @@ def tile_bitlinear_t_kernel(tc, x, weight, bias, out):
                 banks.append(bank)
             return banks
 
-        def evacuate(b, banks):
-            grouped = gpool.tile([P, TILES * D_IN], BF16, name="grouped", align_bytes=64)
-            for t in range(TILES):
+        def evacuate(b, tiles, banks):
+            if tiles[0] == 0:
+                grouped = gpool.tile([P, TILES * D_IN], BF16, name="grouped", align_bytes=64)
+                grouped_tiles[b] = grouped
+            grouped = grouped_tiles[b]
+            for t, bank in zip(tiles, banks):
                 dst = grouped[:, t * D_IN : (t + 1) * D_IN].bitcast(F32).rearrange("p (g r u) -> p g r u", g=PASSES, u=2)
-                src = banks[t][:].rearrange("p (g u r) -> p g r u", g=PASSES, u=2)
+                src = bank[:].rearrange("p (g u r) -> p g r u", g=PASSES, u=2)
                 nc.scalar.copy(out=dst, in_=src)
-            grouped_tiles[b] = grouped
 
         def quantise(b):
             codes = cpool.tile([P, TILES * PASSES * P], U32, name="codes", align_bytes=64)
@@ -198,10 +201,10 @@ def tile_bitlinear_t_kernel(tc, x, weight, bias, out):
                     in_=w_grouped[:, 4 * lo : 4 * (lo + P)],
                 )
 
-        def multiply(i):
+        def multiply(i, tiles):
             codes, scales = code_tiles[i]
             banks = []
-            for t in range(TILES):
+            for t in tiles:
                 acc = psum.tile([P, D_OUT], F32, name="acc", tag="bank")
                 for g in range(PASSES):
                     cols = slice((t * PASSES + g) * P, (t * PASSES + g + 1) * P)
@@ -230,16 +233,38 @@ def tile_bitlinear_t_kernel(tc, x, weight, bias, out):
         next_q = 0
         for s in range(BUNCHES + LAG):
             i = s - LAG
-            if s < BUNCHES:
-                banks = transposes(s)
-                if s + X_BUFS < BUNCHES:
-                    load(s + X_BUFS, 1)
-                evacuate(s, banks)
+            both = s < BUNCHES and i >= 0
+            parts = [list(range(h, h + GRAN)) for h in range(0, TILES, GRAN)] if both else [list(range(TILES))]
+            last = i == BUNCHES - 1
+            if i >= 0:
+                for n in range(2):
+                    if next_q < min(s, BUNCHES):
+                        quantise(next_q)
+                        next_q += 1
+                result = opool.tile([P, TILES, D_OUT], F32, name="result")
+            for tiles in parts:
+                if s < BUNCHES:
+                    banks = transposes(s, tiles)
+                    if tiles[-1] == TILES - 1 and s + X_BUFS < BUNCHES:
+                        load(s + X_BUFS, 1)
+                    evacuate(s, tiles, banks)
+                if i >= 0:
+                    accs = multiply(i, tiles)
+                    for t, acc in zip(tiles, accs):
+                        if t < POOL_TILES:
+                            raw = rpool.tile([P, D_OUT], F32, name="raw")
+                            nc.scalar.copy(out=raw[:], in_=acc[:])
+                            nc.gpsimd.tensor_tensor(out=result[:, t, :], in0=raw[:], in1=bias_all[:], op=ALU.add)
+                        else:
+                            nc.vector.tensor_tensor(out=result[:, t, :], in0=acc[:], in1=bias_all[:], op=ALU.add)
+                        if last:
+                            nc.sync.dma_start(out=out_view(i)[:, t, :], in_=result[:, t, :])
+            if i >= 0 and not last:
+                nc.sync.dma_start(out=out_view(i), in_=result[:])
             if s == 0:
                 bias_bank = psum.tile([P, D_OUT], F32, name="bias_bank", tag="bank")
                 nc.tensor.matmul(out=bias_bank[:], lhsT=ones[:], rhs=bias_pad[:], start=True, stop=True)
                 nc.scalar.copy(out=bias_all[:], in_=bias_bank[:])
-            if s == 0:
                 ternary(0)
             for a in range(OUT_TILES):
                 if WT_AFTER[a] == s:
@@ -251,24 +276,5 @@ def tile_bitlinear_t_kernel(tc, x, weight, bias, out):
                         quantise(1)
                         next_q = 2
                     quantise_weights(a)
-            if i >= 0:
-                accs = multiply(i)
-                for n in range(2):
-                    if next_q < min(s, BUNCHES):
-                        quantise(next_q)
-                        next_q += 1
-                result = opool.tile([P, TILES, D_OUT], F32, name="result")
-                last = i == BUNCHES - 1
-                for t in range(TILES):
-                    if t < POOL_TILES:
-                        raw = rpool.tile([P, D_OUT], F32, name="raw")
-                        nc.scalar.copy(out=raw[:], in_=accs[t][:])
-                        nc.gpsimd.tensor_tensor(out=result[:, t, :], in0=raw[:], in1=bias_all[:], op=ALU.add)
-                    else:
-                        nc.vector.tensor_tensor(out=result[:, t, :], in0=accs[t][:], in1=bias_all[:], op=ALU.add)
-                    if last:
-                        nc.sync.dma_start(out=out_view(i)[:, t, :], in_=result[:, t, :])
-                if not last:
-                    nc.sync.dma_start(out=out_view(i), in_=result[:])
             if s + 1 < BUNCHES:
                 sort_words(s + 1)

@@ -35,7 +35,8 @@ X_BUFS = 4
 G_BUFS = LAG + 1
 C_BUFS = LAG + 2
 R_BUFS = 3
-WT_AFTER = (0, 1, 2, 4)
+FINE = 2
+WT_AFTER = (1, 2, 4, 5)
 
 FLOPS = 2 * TOKENS * D_IN * D_OUT
 
@@ -235,7 +236,7 @@ def tile_bitlinear_t_kernel(tc, x, weight, bias, out):
             i = s - LAG
             both = s < BUNCHES and i >= 0
             parts = [list(range(h, h + GRAN)) for h in range(0, TILES, GRAN)] if both else [list(range(TILES))]
-            last = i == BUNCHES - 1
+            last = i >= BUNCHES - FINE
             if i >= 0:
                 for n in range(2):
                     if next_q < min(s, BUNCHES):

@@ -27,16 +27,24 @@ BUNCH = P * TILES
 BUNCHES = TOKENS // BUNCH
 OUT_TILES = D_OUT // P
 
-LAG = 7
-SORTED = 2
+LAG = 6
+PAIR = 2
+WT_AT = (1, 4)
+Q_FROM = 2
+Q_EARLY = 1
+SORTED = (0, 1, 2, 3)
+VECTOR_SORTED = (3,)
+QUANTISE_PART = 0
+QUANTISE_MOST = 2
 POOL_TILES = 1
+POOL_MIXED = 0
 GRAN = 2
+SORT_BUFS = 8
 X_BUFS = 4
-G_BUFS = LAG + 1
+G_BUFS = 6
 C_BUFS = LAG + 2
 R_BUFS = 3
 FINE = 2
-WT_AFTER = (1, 2, 4, 5)
 
 FLOPS = 2 * TOKENS * D_IN * D_OUT
 
@@ -50,9 +58,10 @@ def tile_bitlinear_t_kernel(tc, x, weight, bias, out):
         ctx.enter_context(tc.manual_schedule())
         const = ctx.enter_context(tc.tile_pool(name="const", bufs=1))
         wpool = ctx.enter_context(tc.tile_pool(name="wpool", bufs=1))
-        wtmp = ctx.enter_context(tc.tile_pool(name="wtmp", bufs=2))
+        wtmp = ctx.enter_context(tc.tile_pool(name="wtmp", bufs=1))
+        wqpool = ctx.enter_context(tc.tile_pool(name="wqpool", bufs=OUT_TILES))
         xpool = ctx.enter_context(tc.tile_pool(name="xpool", bufs=X_BUFS))
-        spool = ctx.enter_context(tc.tile_pool(name="spool", bufs=2 * max(SORTED, 1)))
+        spool = ctx.enter_context(tc.tile_pool(name="spool", bufs=SORT_BUFS))
         gpool = ctx.enter_context(tc.tile_pool(name="gpool", bufs=G_BUFS))
         cpool = ctx.enter_context(tc.tile_pool(name="cpool", bufs=C_BUFS))
         opool = ctx.enter_context(tc.tile_pool(name="opool", bufs=R_BUFS))
@@ -61,8 +70,6 @@ def tile_bitlinear_t_kernel(tc, x, weight, bias, out):
 
         ident = const.tile([P, P], F32, name="ident")
         make_identity(nc, ident[:])
-        ident_bf = const.tile([P, P], BF16, name="ident_bf")
-        make_identity(nc, ident_bf[:])
         ones = const.tile([P, P], BF16, name="ones")
         nc.vector.memset(ones[:], 1.0)
         bias_pad = const.tile([P, D_OUT], BF16, name="bias_pad")
@@ -89,13 +96,14 @@ def tile_bitlinear_t_kernel(tc, x, weight, bias, out):
             x_tiles[b] = xs
 
         def is_sorted(b, t):
-            return b > LAG and t >= TILES - SORTED
+            return b > LAG and t in SORTED
 
-        def sort_words(b):
-            for t in range(TILES):
+        def sort_words(b, tiles):
+            for t in tiles:
                 if is_sorted(b, t):
                     xsort = spool.tile([P, WORDS], F32, name="xsort")
-                    nc.scalar.copy(
+                    copy = nc.vector.tensor_copy if t in VECTOR_SORTED else nc.scalar.copy
+                    copy(
                         out=xsort[:].rearrange("p (g u i) -> p g u i", g=PASSES, u=2),
                         in_=x_tiles[b][:, t, :].bitcast(F32).rearrange("p (g i u) -> p g u i", g=PASSES, u=2),
                     )
@@ -134,72 +142,68 @@ def tile_bitlinear_t_kernel(tc, x, weight, bias, out):
 
         w_sb = wpool.tile([P, OUT_TILES, D_IN], BF16, name="w_sb")
         w_view = weight.rearrange("(a p) k -> p a k", p=P)
-        sums = wpool.tile([P, OUT_TILES * GROUPS], F32, name="sums")
-        scl = wpool.tile([P, OUT_TILES * GROUPS], F32, name="scl")
-        thr = wpool.tile([P, OUT_TILES * GROUPS], F32, name="thr")
-        scl2 = wpool.tile([P, OUT_TILES * GROUPS], F32, name="scl2")
         w_grouped = wpool.tile([P, PASSES * D_OUT * 4], BF16, name="w_grouped", align_bytes=64)
         w_codes = wpool.tile([P, PASSES * D_OUT], U32, name="w_codes", align_bytes=64)
         w_scales = wpool.tile([P, PASSES * D_OUT], U8, name="w_scales", align_bytes=64)
-        w_grouped_values = w_grouped[:].rearrange("p (g o t) -> p g o t", g=PASSES, t=4)
+        w_grouped_words = w_grouped[:].bitcast(F32).rearrange("p (g o u) -> p g o u", g=PASSES, u=2)
         wq_tiles = {}
-        wt_banks = {}
 
-        def load_weights(a):
-            nc.sync.dma_start(out=w_sb[:, a, :], in_=w_view[:, a, :])
+        def load_weights(pair):
+            these = slice(PAIR * pair, PAIR * (pair + 1))
+            nc.sync.dma_start(out=w_sb[:, these, :], in_=w_view[:, these, :])
 
-        def ternary(a):
-            these = slice(a * GROUPS, (a + 1) * GROUPS)
-            mag = wtmp.tile([P, D_IN], BF16, name="mag")
+        def ternary(pair):
+            w_pair = w_sb[:, PAIR * pair : PAIR * (pair + 1), :].rearrange("p a k -> p (a k)")
+            mag = wtmp.tile([P, PAIR * D_IN], BF16, name="mag")
             nc.vector.tensor_scalar(
-                out=mag[:].bitcast(I32), in0=w_sb[:, a, :].bitcast(I32), scalar1=0x7FFF7FFF, scalar2=None, op0=ALU.bitwise_and
+                out=mag[:].bitcast(I32), in0=w_pair.bitcast(I32), scalar1=0x7FFF7FFF, scalar2=None, op0=ALU.bitwise_and
             )
-            nc.vector.tensor_reduce(
-                out=sums[:, these], in_=mag[:].rearrange("p (j i) -> p j i", j=GROUPS), axis=AX.X, op=ALU.add
-            )
+            half_sign = wtmp.tile([P, PAIR * D_IN], BF16, name="half_sign")
             nc.vector.tensor_scalar(
-                out=scl[:, these], in0=sums[:, these], scalar1=1.0 / GROUP, scalar2=EPS, op0=ALU.mult, op1=ALU.max
+                out=half_sign[:], in0=w_pair, scalar1=0.0, scalar2=0.5, op0=ALU.is_ge, op1=ALU.subtract
             )
-            nc.vector.tensor_scalar(out=thr[:, these], in0=scl[:, these], scalar1=0.5, scalar2=None, op0=ALU.mult)
-            nc.vector.tensor_scalar(out=scl2[:, these], in0=scl[:, these], scalar1=2.0, scalar2=None, op0=ALU.mult)
-            half_sign = wtmp.tile([P, D_IN], BF16, name="half_sign")
+            sums = wtmp.tile([P, PAIR * GROUPS], F32, name="sums")
+            nc.vector.tensor_reduce(out=sums[:], in_=mag[:].rearrange("p (j i) -> p j i", i=GROUP), axis=AX.X, op=ALU.add)
+            thr = wtmp.tile([P, PAIR * GROUPS], F32, name="thr")
             nc.vector.tensor_scalar(
-                out=half_sign[:], in0=w_sb[:, a, :], scalar1=0.0, scalar2=0.5, op0=ALU.is_ge, op1=ALU.subtract
+                out=thr[:], in0=sums[:], scalar1=0.5 / GROUP, scalar2=0.5 * EPS, op0=ALU.mult, op1=ALU.max
             )
-            kept = wtmp.tile([P, D_IN], BF16, name="kept")
-            for j in range(GROUPS):
-                c = a * GROUPS + j
+            scl2 = wtmp.tile([P, PAIR * GROUPS], F32, name="scl2")
+            nc.vector.tensor_scalar(
+                out=scl2[:], in0=sums[:], scalar1=2.0 / GROUP, scalar2=2.0 * EPS, op0=ALU.mult, op1=ALU.max
+            )
+            kept = wtmp.tile([P, PAIR * D_IN], BF16, name="kept")
+            for j in range(PAIR * GROUPS):
                 cols = slice(j * GROUP, (j + 1) * GROUP)
                 nc.vector.tensor_scalar(
-                    out=kept[:, cols], in0=mag[:, cols], scalar1=thr[:, c : c + 1], scalar2=scl2[:, c : c + 1],
+                    out=kept[:, cols], in0=mag[:, cols], scalar1=thr[:, j : j + 1], scalar2=scl2[:, j : j + 1],
                     op0=ALU.is_gt, op1=ALU.mult,
                 )
-            wq = wtmp.tile([P, D_IN], BF16, name="wq")
-            nc.vector.tensor_tensor(
-                out=wq[:].rearrange("p (g t i) -> p g t i", g=PASSES, t=4),
-                in0=kept[:].rearrange("p (g i t) -> p g t i", g=PASSES, t=4),
-                in1=half_sign[:].rearrange("p (g i t) -> p g t i", g=PASSES, t=4),
-                op=ALU.mult,
-            )
-            wq_tiles[a] = wq
+            for a in range(PAIR):
+                cols = slice(a * D_IN, (a + 1) * D_IN)
+                wq = wqpool.tile([P, D_IN], BF16, name="wq")
+                nc.vector.tensor_tensor(out=wq[:], in0=kept[:, cols], in1=half_sign[:, cols], op=ALU.mult)
+                wq_tiles[PAIR * pair + a] = wq
 
-        def transpose_weights(a):
-            wt = psum.tile([P, D_IN], BF16, name="wt", tag="bank")
-            for plane in range(PASSES * 4):
-                cols = slice(plane * P, (plane + 1) * P)
-                nc.tensor.transpose(wt[:, cols], wq_tiles[a][:, cols], ident_bf[:])
-            nc.scalar.copy(
-                out=w_grouped_values[:, :, a * P : (a + 1) * P, :],
-                in_=wt[:].rearrange("p (g t r) -> p g r t", g=PASSES, t=4),
-            )
+        def transpose_weights(pair):
+            for a in range(PAIR * pair, PAIR * (pair + 1)):
+                wt = psum.tile([P, WORDS], F32, name="wt", tag="bank")
+                planes = wq_tiles[a][:].bitcast(F32).rearrange("p (g i u) -> p g u i", g=PASSES, u=2)
+                for g in range(PASSES):
+                    for u in range(2):
+                        plane = 2 * g + u
+                        nc.tensor.transpose(wt[:, plane * P : (plane + 1) * P], planes[:, g, u, :], ident[:])
+                nc.scalar.copy(
+                    out=w_grouped_words[:, :, a * P : (a + 1) * P, :],
+                    in_=wt[:].rearrange("p (g u r) -> p g r u", g=PASSES, u=2),
+                )
 
-        def quantise_weights(a):
+        def quantise_weights(pair):
             for g in range(PASSES):
-                lo = g * D_OUT + a * P
+                lo = g * D_OUT + PAIR * pair * P
+                hi = lo + PAIR * P
                 nc.vector.quantize_mx(
-                    out=w_codes[:, lo : lo + P].bitcast(FP8X4),
-                    scales=w_scales[:, lo : lo + P],
-                    in_=w_grouped[:, 4 * lo : 4 * (lo + P)],
+                    out=w_codes[:, lo:hi].bitcast(FP8X4), scales=w_scales[:, lo:hi], in_=w_grouped[:, 4 * lo : 4 * hi]
                 )
 
         def multiply(i, tiles):
@@ -224,12 +228,10 @@ def tile_bitlinear_t_kernel(tc, x, weight, bias, out):
 
         load_weights(0)
         load(0, TILES)
-        load_weights(1)
         load(1, 1)
-        load_weights(2)
-        load(2, 1)
-        load_weights(3)
-        load(3, 1)
+        load_weights(1)
+        for b in range(2, X_BUFS):
+            load(b, 1)
 
         next_q = 0
         for s in range(BUNCHES + LAG):
@@ -238,12 +240,13 @@ def tile_bitlinear_t_kernel(tc, x, weight, bias, out):
             parts = [list(range(h, h + GRAN)) for h in range(0, TILES, GRAN)] if both else [list(range(TILES))]
             last = i >= BUNCHES - FINE
             if i >= 0:
-                for n in range(2):
-                    if next_q < min(s, BUNCHES):
-                        quantise(next_q)
-                        next_q += 1
                 result = opool.tile([P, TILES, D_OUT], F32, name="result")
-            for tiles in parts:
+            for part, tiles in enumerate(parts):
+                if i >= 0 and part == min(QUANTISE_PART, len(parts) - 1):
+                    for n in range(QUANTISE_MOST):
+                        if next_q < min(s, BUNCHES):
+                            quantise(next_q)
+                            next_q += 1
                 if s < BUNCHES:
                     banks = transposes(s, tiles)
                     if tiles[-1] == TILES - 1 and s + X_BUFS < BUNCHES:
@@ -252,7 +255,7 @@ def tile_bitlinear_t_kernel(tc, x, weight, bias, out):
                 if i >= 0:
                     accs = multiply(i, tiles)
                     for t, acc in zip(tiles, accs):
-                        if t < POOL_TILES:
+                        if t < (POOL_MIXED if both else POOL_TILES):
                             raw = rpool.tile([P, D_OUT], F32, name="raw")
                             nc.scalar.copy(out=raw[:], in_=acc[:])
                             nc.gpsimd.tensor_tensor(out=result[:, t, :], in0=raw[:], in1=bias_all[:], op=ALU.add)
@@ -260,22 +263,23 @@ def tile_bitlinear_t_kernel(tc, x, weight, bias, out):
                             nc.vector.tensor_tensor(out=result[:, t, :], in0=acc[:], in1=bias_all[:], op=ALU.add)
                         if last:
                             nc.sync.dma_start(out=out_view(i)[:, t, :], in_=result[:, t, :])
+                if s + 1 < BUNCHES:
+                    sort_words(s + 1, tiles)
             if i >= 0 and not last:
                 nc.sync.dma_start(out=out_view(i), in_=result[:])
-            if s == 0:
+            if s == 2:
                 bias_bank = psum.tile([P, D_OUT], F32, name="bias_bank", tag="bank")
                 nc.tensor.matmul(out=bias_bank[:], lhsT=ones[:], rhs=bias_pad[:], start=True, stop=True)
                 nc.scalar.copy(out=bias_all[:], in_=bias_bank[:])
+            if s == 0:
                 ternary(0)
-            for a in range(OUT_TILES):
-                if WT_AFTER[a] == s:
-                    transpose_weights(a)
-                    if a + 1 < OUT_TILES:
-                        ternary(a + 1)
-                    else:
-                        quantise(0)
-                        quantise(1)
-                        next_q = 2
-                    quantise_weights(a)
-            if s + 1 < BUNCHES:
-                sort_words(s + 1)
+                ternary(1)
+            for pair in range(OUT_TILES // PAIR):
+                if s == WT_AT[pair]:
+                    transpose_weights(pair)
+                    quantise_weights(pair)
+            if Q_FROM <= s < LAG:
+                for n in range(Q_EARLY):
+                    if next_q < s:
+                        quantise(next_q)
+                        next_q += 1

@@ -27,23 +27,24 @@ BUNCH = P * TILES
 BUNCHES = TOKENS // BUNCH
 OUT_TILES = D_OUT // P
 
-LAG = 6
+LAG = 7
 PAIR = 2
-WT_AT = (1, 4)
+WT_AT = (2, 4)
 Q_FROM = 2
-Q_EARLY = 1
-SORTED = (0, 1, 2, 3)
-VECTOR_SORTED = (3,)
+Q_EARLY = 2
+SORTED = (1, 2, 3)
 QUANTISE_PART = 0
+SORT_AHEAD = 1
 QUANTISE_MOST = 2
 POOL_TILES = 1
-POOL_MIXED = 0
 GRAN = 2
-SORT_BUFS = 8
+SORT_BUFS = 6
 X_BUFS = 4
 G_BUFS = 6
 C_BUFS = LAG + 2
-R_BUFS = 3
+R_BUFS = 4
+PIECES = 2
+SPLIT = 8
 FINE = 2
 
 FLOPS = 2 * TOKENS * D_IN * D_OUT
@@ -59,6 +60,7 @@ def tile_bitlinear_t_kernel(tc, x, weight, bias, out):
         const = ctx.enter_context(tc.tile_pool(name="const", bufs=1))
         wpool = ctx.enter_context(tc.tile_pool(name="wpool", bufs=1))
         wtmp = ctx.enter_context(tc.tile_pool(name="wtmp", bufs=1))
+        magpool = ctx.enter_context(tc.tile_pool(name="magpool", bufs=2))
         wqpool = ctx.enter_context(tc.tile_pool(name="wqpool", bufs=OUT_TILES))
         xpool = ctx.enter_context(tc.tile_pool(name="xpool", bufs=X_BUFS))
         spool = ctx.enter_context(tc.tile_pool(name="spool", bufs=SORT_BUFS))
@@ -102,8 +104,7 @@ def tile_bitlinear_t_kernel(tc, x, weight, bias, out):
             for t in tiles:
                 if is_sorted(b, t):
                     xsort = spool.tile([P, WORDS], F32, name="xsort")
-                    copy = nc.vector.tensor_copy if t in VECTOR_SORTED else nc.scalar.copy
-                    copy(
+                    nc.scalar.copy(
                         out=xsort[:].rearrange("p (g u i) -> p g u i", g=PASSES, u=2),
                         in_=x_tiles[b][:, t, :].bitcast(F32).rearrange("p (g i u) -> p g u i", g=PASSES, u=2),
                     )
@@ -149,19 +150,32 @@ def tile_bitlinear_t_kernel(tc, x, weight, bias, out):
         wq_tiles = {}
 
         def load_weights(pair):
-            these = slice(PAIR * pair, PAIR * (pair + 1))
-            nc.sync.dma_start(out=w_sb[:, these, :], in_=w_view[:, these, :])
+            for a in range(PAIR * pair, PAIR * (pair + 1)):
+                nc.sync.dma_start(out=w_sb[:, a, :], in_=w_view[:, a, :])
 
-        def ternary(pair):
-            w_pair = w_sb[:, PAIR * pair : PAIR * (pair + 1), :].rearrange("p a k -> p (a k)")
-            mag = wtmp.tile([P, PAIR * D_IN], BF16, name="mag")
-            nc.vector.tensor_scalar(
-                out=mag[:].bitcast(I32), in0=w_pair.bitcast(I32), scalar1=0x7FFF7FFF, scalar2=None, op0=ALU.bitwise_and
-            )
+        magnitudes = {}
+        half_signs = {}
+
+        def magnitude(pair):
+            mag = magpool.tile([P, PAIR * D_IN], BF16, name="mag")
+            for a in range(PAIR):
+                nc.vector.tensor_scalar(
+                    out=mag[:, a * D_IN : (a + 1) * D_IN].bitcast(I32), in0=w_sb[:, PAIR * pair + a, :].bitcast(I32),
+                    scalar1=0x7FFF7FFF, scalar2=None, op0=ALU.bitwise_and,
+                )
+            magnitudes[pair] = mag
+
+        def signs(pair):
             half_sign = wtmp.tile([P, PAIR * D_IN], BF16, name="half_sign")
-            nc.vector.tensor_scalar(
-                out=half_sign[:], in0=w_pair, scalar1=0.0, scalar2=0.5, op0=ALU.is_ge, op1=ALU.subtract
+            nc.vector.memset(half_sign[:, 0:2], 0.0)
+            nc.gpsimd.tensor_scalar(
+                out=half_sign[:], in0=w_sb[:, PAIR * pair : PAIR * (pair + 1), :].rearrange("p a k -> p (a k)"),
+                scalar1=0.0, scalar2=0.5, op0=ALU.is_ge, op1=ALU.subtract,
             )
+            half_signs[pair] = half_sign
+
+        def keep(pair):
+            mag = magnitudes[pair]
             sums = wtmp.tile([P, PAIR * GROUPS], F32, name="sums")
             nc.vector.tensor_reduce(out=sums[:], in_=mag[:].rearrange("p (j i) -> p j i", i=GROUP), axis=AX.X, op=ALU.add)
             thr = wtmp.tile([P, PAIR * GROUPS], F32, name="thr")
@@ -179,10 +193,13 @@ def tile_bitlinear_t_kernel(tc, x, weight, bias, out):
                     out=kept[:, cols], in0=mag[:, cols], scalar1=thr[:, j : j + 1], scalar2=scl2[:, j : j + 1],
                     op0=ALU.is_gt, op1=ALU.mult,
                 )
+            return kept
+
+        def sign_kept(pair, kept):
             for a in range(PAIR):
                 cols = slice(a * D_IN, (a + 1) * D_IN)
                 wq = wqpool.tile([P, D_IN], BF16, name="wq")
-                nc.vector.tensor_tensor(out=wq[:], in0=kept[:, cols], in1=half_sign[:, cols], op=ALU.mult)
+                nc.vector.tensor_tensor(out=wq[:], in0=kept[:, cols], in1=half_signs[pair][:, cols], op=ALU.mult)
                 wq_tiles[PAIR * pair + a] = wq
 
         def transpose_weights(pair):
@@ -228,10 +245,10 @@ def tile_bitlinear_t_kernel(tc, x, weight, bias, out):
 
         load_weights(0)
         load(0, TILES)
-        load(1, 1)
+        load(1, PIECES)
         load_weights(1)
         for b in range(2, X_BUFS):
-            load(b, 1)
+            load(b, PIECES if b < SPLIT else 1)
 
         next_q = 0
         for s in range(BUNCHES + LAG):
@@ -250,12 +267,12 @@ def tile_bitlinear_t_kernel(tc, x, weight, bias, out):
                 if s < BUNCHES:
                     banks = transposes(s, tiles)
                     if tiles[-1] == TILES - 1 and s + X_BUFS < BUNCHES:
-                        load(s + X_BUFS, 1)
+                        load(s + X_BUFS, PIECES if s + X_BUFS < SPLIT else 1)
                     evacuate(s, tiles, banks)
                 if i >= 0:
                     accs = multiply(i, tiles)
                     for t, acc in zip(tiles, accs):
-                        if t < (POOL_MIXED if both else POOL_TILES):
+                        if t < (0 if both else POOL_TILES):
                             raw = rpool.tile([P, D_OUT], F32, name="raw")
                             nc.scalar.copy(out=raw[:], in_=acc[:])
                             nc.gpsimd.tensor_tensor(out=result[:, t, :], in0=raw[:], in1=bias_all[:], op=ALU.add)
@@ -263,8 +280,8 @@ def tile_bitlinear_t_kernel(tc, x, weight, bias, out):
                             nc.vector.tensor_tensor(out=result[:, t, :], in0=acc[:], in1=bias_all[:], op=ALU.add)
                         if last:
                             nc.sync.dma_start(out=out_view(i)[:, t, :], in_=result[:, t, :])
-                if s + 1 < BUNCHES:
-                    sort_words(s + 1, tiles)
+                if s + SORT_AHEAD < BUNCHES:
+                    sort_words(s + SORT_AHEAD, tiles)
             if i >= 0 and not last:
                 nc.sync.dma_start(out=out_view(i), in_=result[:])
             if s == 2:
@@ -272,8 +289,14 @@ def tile_bitlinear_t_kernel(tc, x, weight, bias, out):
                 nc.tensor.matmul(out=bias_bank[:], lhsT=ones[:], rhs=bias_pad[:], start=True, stop=True)
                 nc.scalar.copy(out=bias_all[:], in_=bias_bank[:])
             if s == 0:
-                ternary(0)
-                ternary(1)
+                magnitude(0)
+                signs(0)
+                kept = keep(0)
+                magnitude(1)
+                sign_kept(0, kept)
+                signs(1)
+                kept = keep(1)
+                sign_kept(1, kept)
             for pair in range(OUT_TILES // PAIR):
                 if s == WT_AT[pair]:
                     transpose_weights(pair)

@@ -27,15 +27,16 @@ BUNCH = P * TILES
 BUNCHES = TOKENS // BUNCH
 OUT_TILES = D_OUT // P
 
-LAG = 7
+LAG = 6
 PAIR = 2
 WT_AT = (2, 4)
 Q_FROM = 2
-Q_EARLY = 2
+Q_EARLY = 1
 SORTED = (1, 2, 3)
 QUANTISE_PART = 0
 SORT_AHEAD = 1
-QUANTISE_MOST = 2
+Q_DOUBLE = 3
+Q_CAP = 2
 POOL_TILES = 1
 GRAN = 2
 SORT_BUFS = 6
@@ -167,8 +168,7 @@ def tile_bitlinear_t_kernel(tc, x, weight, bias, out):
 
         def signs(pair):
             half_sign = wtmp.tile([P, PAIR * D_IN], BF16, name="half_sign")
-            nc.vector.memset(half_sign[:, 0:2], 0.0)
-            nc.gpsimd.tensor_scalar(
+            nc.vector.tensor_scalar(
                 out=half_sign[:], in0=w_sb[:, PAIR * pair : PAIR * (pair + 1), :].rearrange("p a k -> p (a k)"),
                 scalar1=0.0, scalar2=0.5, op0=ALU.is_ge, op1=ALU.subtract,
             )
@@ -260,7 +260,7 @@ def tile_bitlinear_t_kernel(tc, x, weight, bias, out):
                 result = opool.tile([P, TILES, D_OUT], F32, name="result")
             for part, tiles in enumerate(parts):
                 if i >= 0 and part == min(QUANTISE_PART, len(parts) - 1):
-                    for n in range(QUANTISE_MOST):
+                    for n in range(2 if i % Q_DOUBLE == 0 else 1):
                         if next_q < min(s, BUNCHES):
                             quantise(next_q)
                             next_q += 1
@@ -303,6 +303,6 @@ def tile_bitlinear_t_kernel(tc, x, weight, bias, out):
                     quantise_weights(pair)
             if Q_FROM <= s < LAG:
                 for n in range(Q_EARLY):
-                    if next_q < s:
+                    if next_q < min(s, Q_CAP):
                         quantise(next_q)
                         next_q += 1

@@ -29,16 +29,20 @@ OUT_TILES = D_OUT // P
 
 LAG = 6
 PAIR = 2
-WT_AT = (2, 4)
+WT_AT = (1, 4)
 Q_FROM = 2
 Q_EARLY = 1
 SORTED = (1, 2, 3)
 QUANTISE_PART = 0
 SORT_AHEAD = 1
-Q_DOUBLE = 3
+SORT_FROM = LAG + 1
+Q_DOUBLE = 2
 Q_CAP = 2
 POOL_TILES = 1
 GRAN = 2
+POOL_MIXED = 1
+POOL_EVERY = 2
+VECTOR_SORTED = (3,)
 SORT_BUFS = 6
 X_BUFS = 4
 G_BUFS = 6
@@ -99,13 +103,14 @@ def tile_bitlinear_t_kernel(tc, x, weight, bias, out):
             x_tiles[b] = xs
 
         def is_sorted(b, t):
-            return b > LAG and t in SORTED
+            return b >= SORT_FROM and t in SORTED
 
         def sort_words(b, tiles):
             for t in tiles:
                 if is_sorted(b, t):
                     xsort = spool.tile([P, WORDS], F32, name="xsort")
-                    nc.scalar.copy(
+                    copy = nc.vector.tensor_copy if t in VECTOR_SORTED else nc.scalar.copy
+                    copy(
                         out=xsort[:].rearrange("p (g u i) -> p g u i", g=PASSES, u=2),
                         in_=x_tiles[b][:, t, :].bitcast(F32).rearrange("p (g i u) -> p g u i", g=PASSES, u=2),
                     )
@@ -166,18 +171,19 @@ def tile_bitlinear_t_kernel(tc, x, weight, bias, out):
                 )
             magnitudes[pair] = mag
 
-        def signs(pair):
-            half_sign = wtmp.tile([P, PAIR * D_IN], BF16, name="half_sign")
+        def signs(pair, a):
+            if a == 0:
+                half_signs[pair] = wtmp.tile([P, PAIR * D_IN], BF16, name="half_sign")
             nc.vector.tensor_scalar(
-                out=half_sign[:], in0=w_sb[:, PAIR * pair : PAIR * (pair + 1), :].rearrange("p a k -> p (a k)"),
+                out=half_signs[pair][:, a * D_IN : (a + 1) * D_IN], in0=w_sb[:, PAIR * pair + a, :],
                 scalar1=0.0, scalar2=0.5, op0=ALU.is_ge, op1=ALU.subtract,
             )
-            half_signs[pair] = half_sign
 
         def keep(pair):
             mag = magnitudes[pair]
             sums = wtmp.tile([P, PAIR * GROUPS], F32, name="sums")
             nc.vector.tensor_reduce(out=sums[:], in_=mag[:].rearrange("p (j i) -> p j i", i=GROUP), axis=AX.X, op=ALU.add)
+            signs(pair, 0)
             thr = wtmp.tile([P, PAIR * GROUPS], F32, name="thr")
             nc.vector.tensor_scalar(
                 out=thr[:], in0=sums[:], scalar1=0.5 / GROUP, scalar2=0.5 * EPS, op0=ALU.mult, op1=ALU.max
@@ -186,6 +192,7 @@ def tile_bitlinear_t_kernel(tc, x, weight, bias, out):
             nc.vector.tensor_scalar(
                 out=scl2[:], in0=sums[:], scalar1=2.0 / GROUP, scalar2=2.0 * EPS, op0=ALU.mult, op1=ALU.max
             )
+            signs(pair, 1)
             kept = wtmp.tile([P, PAIR * D_IN], BF16, name="kept")
             for j in range(PAIR * GROUPS):
                 cols = slice(j * GROUP, (j + 1) * GROUP)
@@ -272,7 +279,7 @@ def tile_bitlinear_t_kernel(tc, x, weight, bias, out):
                 if i >= 0:
                     accs = multiply(i, tiles)
                     for t, acc in zip(tiles, accs):
-                        if t < (0 if both else POOL_TILES):
+                        if t < (POOL_MIXED * (i % POOL_EVERY == 0) if both else POOL_TILES):
                             raw = rpool.tile([P, D_OUT], F32, name="raw")
                             nc.scalar.copy(out=raw[:], in_=acc[:])
                             nc.gpsimd.tensor_tensor(out=result[:, t, :], in0=raw[:], in1=bias_all[:], op=ALU.add)
@@ -289,14 +296,9 @@ def tile_bitlinear_t_kernel(tc, x, weight, bias, out):
                 nc.tensor.matmul(out=bias_bank[:], lhsT=ones[:], rhs=bias_pad[:], start=True, stop=True)
                 nc.scalar.copy(out=bias_all[:], in_=bias_bank[:])
             if s == 0:
-                magnitude(0)
-                signs(0)
-                kept = keep(0)
-                magnitude(1)
-                sign_kept(0, kept)
-                signs(1)
-                kept = keep(1)
-                sign_kept(1, kept)
+                for pair in range(OUT_TILES // PAIR):
+                    magnitude(pair)
+                    sign_kept(pair, keep(pair))
             for pair in range(OUT_TILES // PAIR):
                 if s == WT_AT[pair]:
                     transpose_weights(pair)

@@ -32,25 +32,25 @@ PAIR = 2
 WT_AT = (1, 4)
 Q_FROM = 2
 Q_EARLY = 1
-SORTED = (1, 2, 3)
+SORTED = (0, 1, 2, 3)
 QUANTISE_PART = 0
 SORT_AHEAD = 1
 SORT_FROM = LAG + 1
-Q_DOUBLE = 2
-Q_CAP = 2
+Q_DOUBLE = 4
+Q_CAP = 4
 POOL_TILES = 1
+LAST = (BUNCHES - 1, TILES - 1)
 GRAN = 2
-POOL_MIXED = 1
-POOL_EVERY = 2
 VECTOR_SORTED = (3,)
-SORT_BUFS = 6
+SORT_BUFS = 8
 X_BUFS = 4
 G_BUFS = 6
 C_BUFS = LAG + 2
 R_BUFS = 4
 PIECES = 2
 SPLIT = 8
-FINE = 2
+FINE = 1
+HALF = BUNCHES
 
 FLOPS = 2 * TOKENS * D_IN * D_OUT
 
@@ -81,7 +81,6 @@ def tile_bitlinear_t_kernel(tc, x, weight, bias, out):
         nc.vector.memset(ones[:], 1.0)
         bias_pad = const.tile([P, D_OUT], BF16, name="bias_pad")
         nc.vector.memset(bias_pad[:], 0.0)
-        nc.scalar.dma_start(out=bias_pad[0:1, :], in_=bias.rearrange("(o n) -> o n", o=1))
         bias_all = const.tile([P, D_OUT], F32, name="bias_all")
 
         x_tiles = {}
@@ -94,6 +93,9 @@ def tile_bitlinear_t_kernel(tc, x, weight, bias, out):
 
         def out_view(b):
             return out_rows[b * BUNCH : (b + 1) * BUNCH, :].rearrange("(p t) n -> p t n", t=TILES)
+
+        def store_tiles(i):
+            return 1 if i >= BUNCHES - FINE else 2 if i >= BUNCHES - HALF else TILES
 
         def load(b, pieces):
             xs = xpool.tile([P, TILES, D_IN], BF16, name="xs")
@@ -230,39 +232,64 @@ def tile_bitlinear_t_kernel(tc, x, weight, bias, out):
                     out=w_codes[:, lo:hi].bitcast(FP8X4), scales=w_scales[:, lo:hi], in_=w_grouped[:, 4 * lo : 4 * hi]
                 )
 
+        def column_pieces(i, t):
+            pieces = 2 if (i, t) == LAST else 1
+            step = D_OUT // pieces
+            return [slice(lo, lo + step) for lo in range(0, D_OUT, step)]
+
         def multiply(i, tiles):
             codes, scales = code_tiles[i]
             banks = []
             for t in tiles:
                 acc = psum.tile([P, D_OUT], F32, name="acc", tag="bank")
-                for g in range(PASSES):
-                    cols = slice((t * PASSES + g) * P, (t * PASSES + g + 1) * P)
-                    outs = slice(g * D_OUT, (g + 1) * D_OUT)
-                    nc.tensor.matmul_mx(
-                        out=acc[:],
-                        lhsT=codes[:, cols].bitcast(FP8X4),
-                        lhsT_scale=scales[:, cols],
-                        rhs=w_codes[:, outs].bitcast(FP8X4),
-                        rhs_scale=w_scales[:, outs],
-                        start=(g == 0),
-                        stop=(g == PASSES - 1),
-                    )
+                for piece in column_pieces(i, t):
+                    for g in range(PASSES):
+                        cols = slice((t * PASSES + g) * P, (t * PASSES + g + 1) * P)
+                        outs = slice(g * D_OUT + piece.start, g * D_OUT + piece.stop)
+                        nc.tensor.matmul_mx(
+                            out=acc[:, piece],
+                            lhsT=codes[:, cols].bitcast(FP8X4),
+                            lhsT_scale=scales[:, cols],
+                            rhs=w_codes[:, outs].bitcast(FP8X4),
+                            rhs_scale=w_scales[:, outs],
+                            start=(g == 0),
+                            stop=(g == PASSES - 1),
+                        )
                 banks.append(acc)
             return banks
 
+        def add_bias(i, t, acc, result, on_gpsimd):
+            if on_gpsimd:
+                raw = rpool.tile([P, D_OUT], F32, name="raw")
+                nc.scalar.copy(out=raw[:], in_=acc[:])
+                nc.gpsimd.tensor_tensor(out=result[:, t, :], in0=raw[:], in1=bias_all[:], op=ALU.add)
+            else:
+                for piece in column_pieces(i, t):
+                    nc.vector.tensor_tensor(out=result[:, t, piece], in0=acc[:, piece], in1=bias_all[:, piece], op=ALU.add)
+
+        def store(i, t, result):
+            n = store_tiles(i)
+            if (t + 1) % n == 0:
+                for piece in column_pieces(i, t):
+                    nc.sync.dma_start(out=out_view(i)[:, t + 1 - n : t + 1, piece], in_=result[:, t + 1 - n : t + 1, piece])
+
         load_weights(0)
+        nc.sync.dma_start(out=bias_pad[0:1, :], in_=bias.rearrange("(o n) -> o n", o=1))
         load(0, TILES)
         load(1, PIECES)
         load_weights(1)
         for b in range(2, X_BUFS):
             load(b, PIECES if b < SPLIT else 1)
 
+        bias_bank = psum.tile([P, D_OUT], F32, name="bias_bank", tag="bank")
+        nc.tensor.matmul(out=bias_bank[:], lhsT=ones[:], rhs=bias_pad[:], start=True, stop=True)
+        nc.scalar.copy(out=bias_all[:], in_=bias_bank[:])
+
         next_q = 0
         for s in range(BUNCHES + LAG):
             i = s - LAG
             both = s < BUNCHES and i >= 0
             parts = [list(range(h, h + GRAN)) for h in range(0, TILES, GRAN)] if both else [list(range(TILES))]
-            last = i >= BUNCHES - FINE
             if i >= 0:
                 result = opool.tile([P, TILES, D_OUT], F32, name="result")
             for part, tiles in enumerate(parts):
@@ -279,32 +306,20 @@ def tile_bitlinear_t_kernel(tc, x, weight, bias, out):
                 if i >= 0:
                     accs = multiply(i, tiles)
                     for t, acc in zip(tiles, accs):
-                        if t < (POOL_MIXED * (i % POOL_EVERY == 0) if both else POOL_TILES):
-                            raw = rpool.tile([P, D_OUT], F32, name="raw")
-                            nc.scalar.copy(out=raw[:], in_=acc[:])
-                            nc.gpsimd.tensor_tensor(out=result[:, t, :], in0=raw[:], in1=bias_all[:], op=ALU.add)
-                        else:
-                            nc.vector.tensor_tensor(out=result[:, t, :], in0=acc[:], in1=bias_all[:], op=ALU.add)
-                        if last:
-                            nc.sync.dma_start(out=out_view(i)[:, t, :], in_=result[:, t, :])
+                        add_bias(i, t, acc, result, on_gpsimd=not both and i < BUNCHES - 1 and t < POOL_TILES)
+                        store(i, t, result)
                 if s + SORT_AHEAD < BUNCHES:
                     sort_words(s + SORT_AHEAD, tiles)
-            if i >= 0 and not last:
-                nc.sync.dma_start(out=out_view(i), in_=result[:])
-            if s == 2:
-                bias_bank = psum.tile([P, D_OUT], F32, name="bias_bank", tag="bank")
-                nc.tensor.matmul(out=bias_bank[:], lhsT=ones[:], rhs=bias_pad[:], start=True, stop=True)
-                nc.scalar.copy(out=bias_all[:], in_=bias_bank[:])
             if s == 0:
                 for pair in range(OUT_TILES // PAIR):
                     magnitude(pair)
                     sign_kept(pair, keep(pair))
-            for pair in range(OUT_TILES // PAIR):
-                if s == WT_AT[pair]:
-                    transpose_weights(pair)
-                    quantise_weights(pair)
             if Q_FROM <= s < LAG:
                 for n in range(Q_EARLY):
                     if next_q < min(s, Q_CAP):
                         quantise(next_q)
                         next_q += 1
+            for pair in range(OUT_TILES // PAIR):
+                if s == WT_AT[pair]:
+                    transpose_weights(pair)
+                    quantise_weights(pair)

from contextlib import ExitStack

import concourse.mybir as mybir
from concourse.masks import make_identity

F32 = mybir.dt.float32
BF16 = mybir.dt.bfloat16
U32 = mybir.dt.uint32
U8 = mybir.dt.uint8
I32 = mybir.dt.int32
FP8X4 = mybir.dt.float8_e4m3fn_x4
ALU = mybir.AluOpType
AX = mybir.AxisListType

P = 128
TOKENS = 4 * 2048
D_IN = 1024
D_OUT = 512
GROUP = 128
GROUPS = D_IN // GROUP
EPS = 1e-8
K_PASS = 4 * P
PASSES = D_IN // K_PASS
WORDS = D_IN // 2
TILES = 4
BUNCH = P * TILES
BUNCHES = TOKENS // BUNCH
OUT_TILES = D_OUT // P

LAG = 6
PAIR = 2
WT_AT = (1, 4)
Q_FROM = 2
Q_EARLY = 1
SORTED = (0, 1, 2, 3)
QUANTISE_PART = 0
SORT_AHEAD = 1
SORT_FROM = LAG + 1
Q_DOUBLE = 4
Q_CAP = 4
POOL_TILES = 1
LAST = (BUNCHES - 1, TILES - 1)
GRAN = 2
VECTOR_SORTED = (3,)
SORT_BUFS = 8
X_BUFS = 4
G_BUFS = 6
C_BUFS = LAG + 2
R_BUFS = 4
PIECES = 2
SPLIT = 8
FINE = 1
HALF = BUNCHES

FLOPS = 2 * TOKENS * D_IN * D_OUT


def tile_bitlinear_t_kernel(tc, x, weight, bias, out):
    nc = tc.nc
    x_rows = x.flatten_outer_dims()
    out_rows = out.flatten_outer_dims()

    with ExitStack() as ctx:
        ctx.enter_context(tc.manual_schedule())
        const = ctx.enter_context(tc.tile_pool(name="const", bufs=1))
        wpool = ctx.enter_context(tc.tile_pool(name="wpool", bufs=1))
        wtmp = ctx.enter_context(tc.tile_pool(name="wtmp", bufs=1))
        magpool = ctx.enter_context(tc.tile_pool(name="magpool", bufs=2))
        wqpool = ctx.enter_context(tc.tile_pool(name="wqpool", bufs=OUT_TILES))
        xpool = ctx.enter_context(tc.tile_pool(name="xpool", bufs=X_BUFS))
        spool = ctx.enter_context(tc.tile_pool(name="spool", bufs=SORT_BUFS))
        gpool = ctx.enter_context(tc.tile_pool(name="gpool", bufs=G_BUFS))
        cpool = ctx.enter_context(tc.tile_pool(name="cpool", bufs=C_BUFS))
        opool = ctx.enter_context(tc.tile_pool(name="opool", bufs=R_BUFS))
        rpool = ctx.enter_context(tc.tile_pool(name="rpool", bufs=2))
        psum = ctx.enter_context(tc.psum_pool(name="psum", bufs=8))

        ident = const.tile([P, P], F32, name="ident")
        make_identity(nc, ident[:])
        ones = const.tile([P, P], BF16, name="ones")
        nc.vector.memset(ones[:], 1.0)
        bias_pad = const.tile([P, D_OUT], BF16, name="bias_pad")
        nc.vector.memset(bias_pad[:], 0.0)
        bias_all = const.tile([P, D_OUT], F32, name="bias_all")

        x_tiles = {}
        sorted_tiles = {}
        grouped_tiles = {}
        code_tiles = {}

        def x_view(b):
            return x_rows[b * BUNCH : (b + 1) * BUNCH, :].rearrange("(p t) k -> p t k", t=TILES)

        def out_view(b):
            return out_rows[b * BUNCH : (b + 1) * BUNCH, :].rearrange("(p t) n -> p t n", t=TILES)

        def store_tiles(i):
            return 1 if i >= BUNCHES - FINE else 2 if i >= BUNCHES - HALF else TILES

        def load(b, pieces):
            xs = xpool.tile([P, TILES, D_IN], BF16, name="xs")
            step = TILES // pieces
            for t in range(0, TILES, step):
                nc.sync.dma_start(out=xs[:, t : t + step, :], in_=x_view(b)[:, t : t + step, :])
            x_tiles[b] = xs

        def is_sorted(b, t):
            return b >= SORT_FROM and t in SORTED

        def sort_words(b, tiles):
            for t in tiles:
                if is_sorted(b, t):
                    xsort = spool.tile([P, WORDS], F32, name="xsort")
                    copy = nc.vector.tensor_copy if t in VECTOR_SORTED else nc.scalar.copy
                    copy(
                        out=xsort[:].rearrange("p (g u i) -> p g u i", g=PASSES, u=2),
                        in_=x_tiles[b][:, t, :].bitcast(F32).rearrange("p (g i u) -> p g u i", g=PASSES, u=2),
                    )
                    sorted_tiles[(b, t)] = xsort

        def transposes(b, tiles):
            banks = []
            for t in tiles:
                bank = psum.tile([P, WORDS], F32, name="bank")
                if is_sorted(b, t):
                    planes = sorted_tiles[(b, t)][:].rearrange("p (g u i) -> p g u i", g=PASSES, u=2)
                else:
                    planes = x_tiles[b][:, t, :].bitcast(F32).rearrange("p (g i u) -> p g u i", g=PASSES, u=2)
                for g in range(PASSES):
                    for u in range(2):
                        plane = 2 * g + u
                        nc.tensor.transpose(bank[:, plane * P : (plane + 1) * P], planes[:, g, u, :], ident[:])
                banks.append(bank)
            return banks

        def evacuate(b, tiles, banks):
            if tiles[0] == 0:
                grouped = gpool.tile([P, TILES * D_IN], BF16, name="grouped", align_bytes=64)
                grouped_tiles[b] = grouped
            grouped = grouped_tiles[b]
            for t, bank in zip(tiles, banks):
                dst = grouped[:, t * D_IN : (t + 1) * D_IN].bitcast(F32).rearrange("p (g r u) -> p g r u", g=PASSES, u=2)
                src = bank[:].rearrange("p (g u r) -> p g r u", g=PASSES, u=2)
                nc.scalar.copy(out=dst, in_=src)

        def quantise(b):
            codes = cpool.tile([P, TILES * PASSES * P], U32, name="codes", align_bytes=64)
            scales = cpool.tile([P, TILES * PASSES * P], U8, name="scales", align_bytes=64)
            nc.vector.quantize_mx(out=codes[:].bitcast(FP8X4), scales=scales[:], in_=grouped_tiles[b][:])
            code_tiles[b] = (codes, scales)

        w_sb = wpool.tile([P, OUT_TILES, D_IN], BF16, name="w_sb")
        w_view = weight.rearrange("(a p) k -> p a k", p=P)
        w_grouped = wpool.tile([P, PASSES * D_OUT * 4], BF16, name="w_grouped", align_bytes=64)
        w_codes = wpool.tile([P, PASSES * D_OUT], U32, name="w_codes", align_bytes=64)
        w_scales = wpool.tile([P, PASSES * D_OUT], U8, name="w_scales", align_bytes=64)
        w_grouped_words = w_grouped[:].bitcast(F32).rearrange("p (g o u) -> p g o u", g=PASSES, u=2)
        wq_tiles = {}

        def load_weights(pair):
            for a in range(PAIR * pair, PAIR * (pair + 1)):
                nc.sync.dma_start(out=w_sb[:, a, :], in_=w_view[:, a, :])

        magnitudes = {}
        half_signs = {}

        def magnitude(pair):
            mag = magpool.tile([P, PAIR * D_IN], BF16, name="mag")
            for a in range(PAIR):
                nc.vector.tensor_scalar(
                    out=mag[:, a * D_IN : (a + 1) * D_IN].bitcast(I32), in0=w_sb[:, PAIR * pair + a, :].bitcast(I32),
                    scalar1=0x7FFF7FFF, scalar2=None, op0=ALU.bitwise_and,
                )
            magnitudes[pair] = mag

        def signs(pair, a):
            if a == 0:
                half_signs[pair] = wtmp.tile([P, PAIR * D_IN], BF16, name="half_sign")
            nc.vector.tensor_scalar(
                out=half_signs[pair][:, a * D_IN : (a + 1) * D_IN], in0=w_sb[:, PAIR * pair + a, :],
                scalar1=0.0, scalar2=0.5, op0=ALU.is_ge, op1=ALU.subtract,
            )

        def keep(pair):
            mag = magnitudes[pair]
            sums = wtmp.tile([P, PAIR * GROUPS], F32, name="sums")
            nc.vector.tensor_reduce(out=sums[:], in_=mag[:].rearrange("p (j i) -> p j i", i=GROUP), axis=AX.X, op=ALU.add)
            signs(pair, 0)
            thr = wtmp.tile([P, PAIR * GROUPS], F32, name="thr")
            nc.vector.tensor_scalar(
                out=thr[:], in0=sums[:], scalar1=0.5 / GROUP, scalar2=0.5 * EPS, op0=ALU.mult, op1=ALU.max
            )
            scl2 = wtmp.tile([P, PAIR * GROUPS], F32, name="scl2")
            nc.vector.tensor_scalar(
                out=scl2[:], in0=sums[:], scalar1=2.0 / GROUP, scalar2=2.0 * EPS, op0=ALU.mult, op1=ALU.max
            )
            signs(pair, 1)
            kept = wtmp.tile([P, PAIR * D_IN], BF16, name="kept")
            for j in range(PAIR * GROUPS):
                cols = slice(j * GROUP, (j + 1) * GROUP)
                nc.vector.tensor_scalar(
                    out=kept[:, cols], in0=mag[:, cols], scalar1=thr[:, j : j + 1], scalar2=scl2[:, j : j + 1],
                    op0=ALU.is_gt, op1=ALU.mult,
                )
            return kept

        def sign_kept(pair, kept):
            for a in range(PAIR):
                cols = slice(a * D_IN, (a + 1) * D_IN)
                wq = wqpool.tile([P, D_IN], BF16, name="wq")
                nc.vector.tensor_tensor(out=wq[:], in0=kept[:, cols], in1=half_signs[pair][:, cols], op=ALU.mult)
                wq_tiles[PAIR * pair + a] = wq

        def transpose_weights(pair):
            for a in range(PAIR * pair, PAIR * (pair + 1)):
                wt = psum.tile([P, WORDS], F32, name="wt", tag="bank")
                planes = wq_tiles[a][:].bitcast(F32).rearrange("p (g i u) -> p g u i", g=PASSES, u=2)
                for g in range(PASSES):
                    for u in range(2):
                        plane = 2 * g + u
                        nc.tensor.transpose(wt[:, plane * P : (plane + 1) * P], planes[:, g, u, :], ident[:])
                nc.scalar.copy(
                    out=w_grouped_words[:, :, a * P : (a + 1) * P, :],
                    in_=wt[:].rearrange("p (g u r) -> p g r u", g=PASSES, u=2),
                )

        def quantise_weights(pair):
            for g in range(PASSES):
                lo = g * D_OUT + PAIR * pair * P
                hi = lo + PAIR * P
                nc.vector.quantize_mx(
                    out=w_codes[:, lo:hi].bitcast(FP8X4), scales=w_scales[:, lo:hi], in_=w_grouped[:, 4 * lo : 4 * hi]
                )

        def column_pieces(i, t):
            pieces = 2 if (i, t) == LAST else 1
            step = D_OUT // pieces
            return [slice(lo, lo + step) for lo in range(0, D_OUT, step)]

        def multiply(i, tiles):
            codes, scales = code_tiles[i]
            banks = []
            for t in tiles:
                acc = psum.tile([P, D_OUT], F32, name="acc", tag="bank")
                for piece in column_pieces(i, t):
                    for g in range(PASSES):
                        cols = slice((t * PASSES + g) * P, (t * PASSES + g + 1) * P)
                        outs = slice(g * D_OUT + piece.start, g * D_OUT + piece.stop)
                        nc.tensor.matmul_mx(
                            out=acc[:, piece],
                            lhsT=codes[:, cols].bitcast(FP8X4),
                            lhsT_scale=scales[:, cols],
                            rhs=w_codes[:, outs].bitcast(FP8X4),
                            rhs_scale=w_scales[:, outs],
                            start=(g == 0),
                            stop=(g == PASSES - 1),
                        )
                banks.append(acc)
            return banks

        def add_bias(i, t, acc, result, on_gpsimd):
            if on_gpsimd:
                raw = rpool.tile([P, D_OUT], F32, name="raw")
                nc.scalar.copy(out=raw[:], in_=acc[:])
                nc.gpsimd.tensor_tensor(out=result[:, t, :], in0=raw[:], in1=bias_all[:], op=ALU.add)
            else:
                for piece in column_pieces(i, t):
                    nc.vector.tensor_tensor(out=result[:, t, piece], in0=acc[:, piece], in1=bias_all[:, piece], op=ALU.add)

        def store(i, t, result):
            n = store_tiles(i)
            if (t + 1) % n == 0:
                for piece in column_pieces(i, t):
                    nc.sync.dma_start(out=out_view(i)[:, t + 1 - n : t + 1, piece], in_=result[:, t + 1 - n : t + 1, piece])

        load_weights(0)
        nc.sync.dma_start(out=bias_pad[0:1, :], in_=bias.rearrange("(o n) -> o n", o=1))
        load(0, TILES)
        load(1, PIECES)
        load_weights(1)
        for b in range(2, X_BUFS):
            load(b, PIECES if b < SPLIT else 1)

        bias_bank = psum.tile([P, D_OUT], F32, name="bias_bank", tag="bank")
        nc.tensor.matmul(out=bias_bank[:], lhsT=ones[:], rhs=bias_pad[:], start=True, stop=True)
        nc.scalar.copy(out=bias_all[:], in_=bias_bank[:])

        next_q = 0
        for s in range(BUNCHES + LAG):
            i = s - LAG
            both = s < BUNCHES and i >= 0
            parts = [list(range(h, h + GRAN)) for h in range(0, TILES, GRAN)] if both else [list(range(TILES))]
            if i >= 0:
                result = opool.tile([P, TILES, D_OUT], F32, name="result")
            for part, tiles in enumerate(parts):
                if i >= 0 and part == min(QUANTISE_PART, len(parts) - 1):
                    for n in range(2 if i % Q_DOUBLE == 0 else 1):
                        if next_q < min(s, BUNCHES):
                            quantise(next_q)
                            next_q += 1
                if s < BUNCHES:
                    banks = transposes(s, tiles)
                    if tiles[-1] == TILES - 1 and s + X_BUFS < BUNCHES:
                        load(s + X_BUFS, PIECES if s + X_BUFS < SPLIT else 1)
                    evacuate(s, tiles, banks)
                if i >= 0:
                    accs = multiply(i, tiles)
                    for t, acc in zip(tiles, accs):
                        add_bias(i, t, acc, result, on_gpsimd=not both and i < BUNCHES - 1 and t < POOL_TILES)
                        store(i, t, result)
                if s + SORT_AHEAD < BUNCHES:
                    sort_words(s + SORT_AHEAD, tiles)
            if s == 0:
                for pair in range(OUT_TILES // PAIR):
                    magnitude(pair)
                    sign_kept(pair, keep(pair))
            if Q_FROM <= s < LAG:
                for n in range(Q_EARLY):
                    if next_q < min(s, Q_CAP):
                        quantise(next_q)
                        next_q += 1
            for pair in range(OUT_TILES // PAIR):
                if s == WT_AT[pair]:
                    transpose_weights(pair)
                    quantise_weights(pair)
